import numpy as np
import ml_dtypes


def mxq(x, axis, fmt="e4m3"):
    dtype, down = {"e4m3": (ml_dtypes.float8_e4m3fn, 7), "e5m2": (ml_dtypes.float8_e5m2, 14)}[fmt]
    v = np.moveaxis(np.asarray(x, np.float32).astype(ml_dtypes.bfloat16).astype(np.float64), axis, -1)
    blocks = v.reshape(v.shape[:-1] + (-1, 32))
    amax = np.abs(blocks).max(-1, keepdims=True)
    byte = np.maximum(np.where(amax > 0, np.frexp(amax)[1] - 1 + 127, 0) - down, 1)
    scale = np.exp2(byte - 127.0)
    codes = (blocks / scale).astype(np.float32).astype(dtype).astype(np.float64)
    return np.moveaxis((codes * scale).reshape(v.shape), -1, axis)


WIDE = False


def mx_kscale(k):
    if not WIDE:
        return np.ones(k)
    levels = np.array([10, -10, 5, -5, 0])
    if k % 512:
        return np.exp2(np.random.permutation(np.resize(levels, k // 32))).repeat(32)
    a = np.empty((k // 512, 16))
    for p in range(k // 512):
        a[p, :8] = np.random.permutation(np.resize(levels, 8))
        for g in range(8):
            far = levels[np.abs(levels - a[p, g]) >= 10]
            a[p, g + 8] = far[np.random.randint(len(far))]
    return np.exp2(a.ravel()).repeat(32)


BF16 = ml_dtypes.bfloat16


def bf(x):
    return np.asarray(x, np.float32).astype(BF16)


def f64(x):
    return np.asarray(x).astype(np.float64)


B, N, C = 64, 12, 512
BN_EPS = 1e-5


def bn(v):
    mean = v.mean(axis=(0, 2), keepdims=True)
    var = v.var(axis=(0, 2), keepdims=True)
    return (v - mean) / np.sqrt(var + BN_EPS)


def sigmoid(v):
    return 1.0 / (1.0 + np.exp(-v))


def softmax(v, axis):
    p = np.exp(v - v.max(axis=axis, keepdims=True))
    return p / p.sum(axis=axis, keepdims=True)


def draw_w(a, f):
    return bf(np.random.standard_normal((C, C)) * a / np.sqrt(C) / f[None, :])


def setup_inputs():
    s, t = mx_kscale(C), mx_kscale(C)
    s, t = s / s.max(), t / t.max()
    return {"x": bf(np.random.standard_normal((B, N, C)) * s),
            "edge": bf(np.random.standard_normal((B, N * N, C)) * t),
            "WA": draw_w(np.sqrt(2.0), s), "WB": draw_w(np.sqrt(2.0), s), "WE": draw_w(np.sqrt(2.0), t),
            "WU": draw_w(0.4, s), "WV": draw_w(0.5 * N, s)}


def reference(x, edge, WA, WB, WE, WU, WV):
    x, edge = f64(x), f64(edge)
    xq = mxq(x, 2, "e4m3")
    Vix = xq @ mxq(f64(WA), 1, "e4m3").T
    Vjx = xq @ mxq(f64(WB), 1, "e4m3").T
    e_proj = mxq(edge, 2, "e4m3") @ mxq(f64(WE), 1, "e4m3").T
    agg = np.repeat(Vix, N, axis=1) + np.tile(Vjx, (1, N, 1)) + e_proj
    edge_out = edge + np.maximum(bn(agg), 0.0)
    e = sigmoid(edge_out).reshape(B, N, N, C)
    e = softmax(e, 2).reshape(B, N * N, C)
    Ujx = np.tile(xq @ mxq(f64(WV), 1, "e4m3").T, (1, N, 1))
    Uix = xq @ mxq(f64(WU), 1, "e4m3").T
    msg = (e * Ujx).reshape(B, N, N, C).sum(axis=2)
    x_new = Uix + msg / N
    x_out = np.maximum(x + bn(x_new), 0.0)
    return x_out, edge_out

@@ -1,0 +1,419 @@
+from contextlib import ExitStack
+
+import concourse.mybir as mybir
+from concourse.masks import make_identity
+
+F32 = mybir.dt.float32
+BF16 = mybir.dt.bfloat16
+U32 = mybir.dt.uint32
+U8 = mybir.dt.uint8
+FP8X4 = mybir.dt.float8_e4m3fn_x4
+ALU = mybir.AluOpType
+ACT = mybir.ActivationFunctionType
+AX = mybir.AxisListType
+
+B, N, C = 64, 12, 512
+BN_EPS = 1e-5
+P = 128
+HALF = N // 2
+CHUNK = 4
+WORDS = C // 2
+Q = C // P
+
+
+def chunk_list():
+    chunks = [(g, j0, CHUNK) for g in range(HALF) for j0 in range(0, N, CHUNK)]
+    g, j0, n = chunks[-1]
+    return chunks[:-1] + [(g, j0, n // 2), (g, j0 + n // 2, n // 4), (g, j0 + 3 * n // 4, n // 4)]
+
+
+CHUNKS = chunk_list()
+
+LOAD, TURN, QUANTISE, MULTIPLY, NORMALISE, GATE, WEIGH, SUM = 5, 3, 2, 1, 0, -1, -2, -3
+MESSAGE, NODE_STATS, NODE_OUT = -4, -5, -6
+U_ROUNDS = range(-WEIGH - 1, -WEIGH - 1 + N // CHUNK)
+
+FLOPS = 2 * (B * N * N + 4 * B * N) * C * C
+
+
+def tile_cols(t, width=P, n=1):
+    return slice(t * width, (t + n) * width)
+
+
+def live(k):
+    return 0 <= k < len(CHUNKS)
+
+
+def node_closed_by(k):
+    if live(k) and CHUNKS[k][1] + CHUNKS[k][2] == N:
+        return CHUNKS[k][0]
+    return None
+
+
+def tile_graphmodel_pa_kernel(tc, x, edge, WA, WB, WE, WU, WV, out_0, out_1):
+    nc = tc.nc
+    edge_rows = edge.rearrange("b (h t) c -> (b h) (t c)", h=2)
+    edge_out_rows = out_1.rearrange("b (h t) c -> (b h) (t c)", h=2)
+    x_rows = x.rearrange("b (h g) c -> (b h) (g c)", h=2)
+    x_out_rows = out_0.rearrange("b (h g) c -> (b h) (g c)", h=2)
+
+    with ExitStack() as ctx:
+        ctx.enter_context(tc.manual_schedule())
+        keep = ctx.enter_context(tc.tile_pool(name="keep", bufs=1))
+        rows_pool = ctx.enter_context(tc.tile_pool(name="rows", bufs=8))
+        grouped_pool = ctx.enter_context(tc.tile_pool(name="grouped", bufs=3))
+        codes_pool = ctx.enter_context(tc.tile_pool(name="codes", bufs=3))
+        eo_pool = ctx.enter_context(tc.tile_pool(name="eo", bufs=4))
+        junk_pool = ctx.enter_context(tc.tile_pool(name="junk", bufs=4))
+        node_pool = ctx.enter_context(tc.tile_pool(name="node", bufs=2))
+        small = ctx.enter_context(tc.tile_pool(name="small", bufs=4))
+        work_ps = ctx.enter_context(tc.psum_pool(name="work_ps", bufs=3))
+        agg_ps = ctx.enter_context(tc.psum_pool(name="agg_ps", bufs=3))
+        sums_ps = ctx.enter_context(tc.psum_pool(name="sums_ps", bufs=1))
+
+        ident = keep.tile([P, P], F32)
+        make_identity(nc, ident[:])
+        parity = keep.tile([P, 2], F32)
+        nc.vector.tensor_reduce(
+            out=parity[:], in_=ident[:].rearrange("p (b h) -> p h b", h=2), axis=AX.X, op=ALU.add
+        )
+        same_half = keep.tile([P, P], F32)
+        nc.vector.tensor_scalar_mul(
+            out=same_half[:].rearrange("p (b h) -> p b h", h=2),
+            in0=parity[:].unsqueeze(1).to_broadcast([P, B, 2]),
+            scalar1=1.0 / (B * C),
+        )
+        minus_half = keep.tile([P, CHUNK], F32)
+        nc.vector.memset(minus_half[:], -0.5)
+
+        def turn(words, n):
+            banks = []
+            for first in range(0, n, 2):
+                m = min(2, n - first)
+                bank = work_ps.tile([P, 2, 2, P], F32, name="turned", tag="work")
+                for a in range(m):
+                    for u in range(2):
+                        start = (first + a) * WORDS
+                        nc.tensor.transpose(bank[:, a, u, :], words[:, start + u : start + WORDS : 2], ident[:])
+                banks.append((bank, first, m))
+            return banks
+
+        def regroup(copy, turned_bank, grouped_words):
+            bank, first, m = turned_bank
+            copy(
+                out=grouped_words[:, tile_cols(first, 2 * P, m)].rearrange(
+                    "p (a r u) -> p a r u", a=m, u=2
+                ),
+                in_=bank[:, :m, :, :].rearrange("p a u r -> p a r u"),
+            )
+
+        def quantise(grouped, operand, cols):
+            nc.vector.quantize_mx(
+                out=operand[0][:, cols].bitcast(FP8X4), scales=operand[1][:, cols], in_=grouped
+            )
+
+        def mx_operand(pool, name, n):
+            codes = pool.tile([P, n * P], U32, align_bytes=64, name="codes_" + name)
+            scales = pool.tile([P, n * P], U8, align_bytes=64, name="scales_" + name)
+            return codes, scales
+
+        def mx_pass(out, left, left_cols, right, right_cols, start, stop):
+            nc.tensor.matmul_mx(
+                out=out,
+                lhsT=left[0][:, left_cols].bitcast(FP8X4),
+                lhsT_scale=left[1][:, left_cols],
+                rhs=right[0][:, right_cols].bitcast(FP8X4),
+                rhs_scale=right[1][:, right_cols],
+                start=start,
+                stop=stop,
+            )
+
+        def load_weight(w):
+            w_rows = rows_pool.tile([P, CHUNK * C], BF16, name="rows")
+            nc.sync.dma_start(
+                out=w_rows[:].rearrange("p (a k) -> p a k", a=Q),
+                in_=w.rearrange("(a p) k -> p a k", p=P),
+            )
+            return w_rows
+
+        rows = {}
+
+        def load(k):
+            g, j0, n = CHUNKS[k]
+            rows[k] = rows_pool.tile([P, CHUNK * C], BF16, name="rows")
+            nc.sync.dma_start(out=rows[k][:, : n * C], in_=edge_rows[:, tile_cols(g * N + j0, C, n)])
+
+        we_rows, wa_rows, wb_rows = load_weight(WE), load_weight(WA), load_weight(WB)
+        x_own = keep.tile([P, HALF * C], BF16)
+        nc.sync.dma_start(out=x_own[:], in_=x_rows)
+        load(0)
+        wv_rows = load_weight(WV)
+        load(1)
+        wu_rows = load_weight(WU)
+
+        def weight_operand(name, w_rows, copy):
+            operand = mx_operand(keep, name, Q)
+            grouped = grouped_pool.tile([P, CHUNK * C], BF16, align_bytes=64, name="grouped")
+            for turned_bank in turn(w_rows[:].bitcast(F32), Q):
+                regroup(copy, turned_bank, grouped[:].bitcast(F32))
+            quantise(grouped[:], operand, slice(0, C))
+            return operand
+
+        we = weight_operand("we", we_rows, nc.scalar.copy)
+        wa = weight_operand("wa", wa_rows, nc.scalar.copy)
+        wb = weight_operand("wb", wb_rows, nc.scalar.copy)
+
+        xi = mx_operand(keep, "xi", HALF)
+        xj = mx_operand(keep, "xj", N)
+        with tc.tile_pool(name="x_stage", bufs=1) as x_stage:
+            xi_grouped = x_stage.tile([P, HALF * C], BF16, align_bytes=64)
+            xj_grouped = x_stage.tile([P, N * C], BF16, align_bytes=64)
+            for turned_bank in turn(x_own[:].bitcast(F32), HALF):
+                regroup(nc.scalar.copy, turned_bank, xi_grouped[:].bitcast(F32))
+                bank, first, m = turned_bank
+                for a in range(m):
+                    by_half = bank[:, a, :, :].rearrange("p u (b h) -> p h b u", h=2)
+                    for h, copy in enumerate((nc.scalar.copy, nc.vector.tensor_copy)):
+                        copy(
+                            out=xj_grouped[:].bitcast(F32)[
+                                :, tile_cols(HALF * h + first + a, 2 * P)
+                            ].rearrange("p (b d u) -> p b d u", d=2, u=2),
+                            in_=by_half[:, h, :, :].unsqueeze(2).to_broadcast([P, B, 2, 2]),
+                        )
+            quantise(xi_grouped[:, : 4 * C], xi, slice(0, 4 * P))
+            quantise(xi_grouped[:, 4 * C :], xi, slice(4 * P, HALF * P))
+            for part in range(N // CHUNK):
+                quantise(xj_grouped[:, tile_cols(part, CHUNK * C)], xj, tile_cols(part, CHUNK * P))
+
+        gate_pool = ctx.enter_context(tc.tile_pool(name="gate", bufs=3))
+
+        u_all = keep.tile([P, N * C], F32)
+        late = {}
+
+        def make_u(part):
+            for j in range(part * CHUNK, (part + 1) * CHUNK):
+                acc = agg_ps.tile([P, C], F32, name="acc", tag="agg")
+                mx_pass(acc[:], xj, tile_cols(j), late["wv"], slice(0, C), True, True)
+                nc.vector.tensor_copy(out=u_all[:, tile_cols(j, C)], in_=acc[:])
+
+        sums, total, avg, mean_sq, rstd = {}, {}, {}, {}, {}
+
+        def moments(src, dst, key, col):
+            nc.scalar.activation(
+                out=dst, in_=src, func=ACT.Identity, accum_out=sums[key][:, 0, col : col + 1]
+            )
+            junk = junk_pool.tile([P, C], BF16, name="junk")
+            nc.scalar.activation(
+                out=junk[:], in_=src, func=ACT.Square, accum_out=sums[key][:, 1, col : col + 1]
+            )
+
+        def mean_over_graphs(key, n):
+            total[key] = work_ps.tile([P, 2, n], F32, name="total", tag="work")
+            nc.tensor.matmul(
+                out=total[key][:].rearrange("p s n -> p (s n)"),
+                lhsT=same_half[:],
+                rhs=sums[key][:].rearrange("p s n -> p (s n)"),
+                start=True,
+                stop=True,
+            )
+
+        def means_to_sbuf(key, n):
+            avg[key] = small.tile([P, 2, n], F32, name="avg")
+            nc.vector.tensor_copy(out=avg[key][:], in_=total[key][:])
+
+        def square_of_mean(key, n):
+            mean_sq[key] = small.tile([P, n], F32, name="mean_sq")
+            nc.vector.tensor_mul(out=mean_sq[key][:], in0=avg[key][:, 0, :], in1=avg[key][:, 0, :])
+
+        def inverse_std(key, n):
+            var_eps = small.tile([P, n], F32, name="var_eps")
+            nc.vector.scalar_tensor_tensor(
+                out=var_eps[:], in0=avg[key][:, 1, :], scalar=BN_EPS, in1=mean_sq[key][:],
+                op0=ALU.add, op1=ALU.subtract,
+            )
+            rstd[key] = small.tile([P, n], F32, name="rstd")
+            nc.gpsimd.tensor_tensor(
+                out=rstd[key][:], in0=var_eps[:], in1=minus_half[:, :n], op=ALU.pow
+            )
+
+        turned, grouped_of, codes_of, eo, gate = {}, {}, {}, {}, {}
+        den_t, num_t = {}, {}
+
+        def turn_chunk(k):
+            turned[k] = turn(rows[k][:].bitcast(F32), CHUNKS[k][2])
+            grouped_of[k] = grouped_pool.tile([P, CHUNK * C], BF16, align_bytes=64, name="grouped")
+
+        def regroup_chunk(k, copy):
+            for turned_bank in turned[k]:
+                regroup(copy, turned_bank, grouped_of[k][:].bitcast(F32))
+
+        def quantise_chunk(k):
+            n = CHUNKS[k][2]
+            codes_of[k] = mx_operand(codes_pool, "edge", CHUNK)
+            quantise(grouped_of[k][:, : n * C], codes_of[k], slice(0, n * P))
+
+        def multiply(k):
+            g, j0, n = CHUNKS[k]
+            eo[k] = eo_pool.tile([P, CHUNK * C], F32, name="eo")
+            sums[k] = small.tile([P, 2, n], F32, name="sums")
+            for t in range(n):
+                acc = agg_ps.tile([P, C], F32, name="acc", tag="agg")
+                mx_pass(acc[:], codes_of[k], tile_cols(t), we, slice(0, C), True, False)
+                mx_pass(acc[:], xi, tile_cols(g), wa, slice(0, C), False, False)
+                mx_pass(acc[:], xj, tile_cols(j0 + t), wb, slice(0, C), False, True)
+                moments(acc[:], eo[k][:, tile_cols(t, C)], k, t)
+
+        def relu_centred(k, t):
+            nc.vector.tensor_scalar(
+                out=eo[k][:, tile_cols(t, C)], in0=eo[k][:, tile_cols(t, C)],
+                scalar1=avg[k][:, 0, t : t + 1], scalar2=0.0, op0=ALU.subtract, op1=ALU.max,
+            )
+
+        def normalise(k):
+            n = CHUNKS[k][2]
+            square_of_mean(k, n)
+            relu_centred(k, 0)
+            inverse_std(k, n)
+            for t in range(1, n):
+                relu_centred(k, t)
+
+        def add_residual(k):
+            g, j0, n = CHUNKS[k]
+            for t in range(n):
+                nc.vector.scalar_tensor_tensor(
+                    out=eo[k][:, tile_cols(t, C)], in0=eo[k][:, tile_cols(t, C)],
+                    scalar=rstd[k][:, t : t + 1], in1=rows[k][:, tile_cols(t, C)],
+                    op0=ALU.mult, op1=ALU.add,
+                )
+            nc.sync.dma_start(
+                out=edge_out_rows[:, tile_cols(g * N + j0, C, n)], in_=eo[k][:, : n * C]
+            )
+
+        def gates(k):
+            half = CHUNKS[k][2] * C // 2
+            gate[k] = gate_pool.tile([P, 2, CHUNK * C], F32, name="gate")
+            for cols in (tile_cols(0, half), tile_cols(1, half)):
+                nc.scalar.activation(out=gate[k][:, 0, cols], in_=eo[k][:, cols], func=ACT.Tanh, scale=0.5)
+            for cols in (tile_cols(0, half), tile_cols(1, half)):
+                nc.scalar.activation(out=gate[k][:, 0, cols], in_=gate[k][:, 0, cols], func=ACT.Exp, scale=0.5)
+
+        def weigh(k):
+            g, j0, n = CHUNKS[k]
+            nc.vector.tensor_mul(
+                out=gate[k][:, 1, : n * C], in0=gate[k][:, 0, : n * C], in1=u_all[:, tile_cols(j0, C, n)]
+            )
+
+        def sum_over_j(k):
+            g, j0, n = CHUNKS[k]
+            if j0 == 0:
+                den_t[g] = sums_ps.tile([P, Q, P], F32, name="den_t")
+                num_t[g] = sums_ps.tile([P, Q, P], F32, name="num_t")
+            for s, total_t in enumerate((den_t[g], num_t[g])):
+                for t in range(n):
+                    for q in range(Q):
+                        nc.tensor.matmul(
+                            out=total_t[:, q, :],
+                            lhsT=gate[k][:, s, t * C + q * P : t * C + (q + 1) * P],
+                            rhs=ident[:],
+                            is_transpose=True,
+                            start=(j0 + t == 0 and q == 0),
+                            stop=(j0 + t == N - 1 and q == Q - 1),
+                        )
+
+        xn_t, xn = {}, {}
+
+        def message(g):
+            uix_t = work_ps.tile([P, Q, P], F32, name="uix_t", tag="work")
+            for q in range(Q):
+                mx_pass(uix_t[:, q, :], late["wu"], tile_cols(q), xi, tile_cols(g), True, True)
+            rden_t = node_pool.tile([P, Q, P], F32, name="rden_t")
+            msg_t = node_pool.tile([P, Q, P], F32, name="msg_t")
+            xn_t[g] = node_pool.tile([P, Q, P], F32, name="xn_t")
+            halves = (slice(0, Q // 2), slice(Q // 2, Q))
+            for qs in halves:
+                nc.vector.reciprocal(out=rden_t[:, qs, :], in_=den_t[g][:, qs, :])
+            for qs in halves:
+                nc.vector.tensor_mul(out=msg_t[:, qs, :], in0=num_t[g][:, qs, :], in1=rden_t[:, qs, :])
+            for qs in halves:
+                nc.vector.scalar_tensor_tensor(
+                    out=xn_t[g][:, qs, :], in0=msg_t[:, qs, :], scalar=1.0 / N, in1=uix_t[:, qs, :],
+                    op0=ALU.mult, op1=ALU.add,
+                )
+
+        def node_moments(g):
+            xn_ps = work_ps.tile([P, C], F32, name="xn_ps", tag="work")
+            for q in range(Q):
+                nc.tensor.transpose(xn_ps[:, tile_cols(q)], xn_t[g][:, q, :], ident[:])
+            sums["node", g] = small.tile([P, 2, 1], F32, name="sums")
+            xn[g] = node_pool.tile([P, C], F32, name="xn")
+            moments(xn_ps[:], xn[g][:], ("node", g), 0)
+
+        def node_residual(g):
+            shift = small.tile([P, 1], F32, name="shift")
+            nc.vector.scalar_tensor_tensor(
+                out=shift[:], in0=avg["node", g][:, 0, :], scalar=-1.0, in1=rstd["node", g][:],
+                op0=ALU.mult, op1=ALU.mult,
+            )
+            nc.vector.scalar_tensor_tensor(
+                out=xn[g][:], in0=xn[g][:], scalar=rstd["node", g][:, 0:1],
+                in1=x_own[:, tile_cols(g, C)], op0=ALU.mult, op1=ALU.add,
+            )
+            return shift
+
+        def node_out(g, shift):
+            xo = node_pool.tile([P, C], F32, name="xo")
+            nc.scalar.activation(out=xo[:], in_=xn[g][:], func=ACT.Relu, bias=shift[:, 0:1], scale=1.0)
+            nc.sync.dma_start(out=x_out_rows[:, tile_cols(g, C)], in_=xo[:])
+
+        for i in range(-TURN, len(CHUNKS) - NODE_OUT):
+            g_message = node_closed_by(i + MESSAGE)
+            g_stats = node_closed_by(i + NODE_STATS)
+            g_out = node_closed_by(i + NODE_OUT)
+            shift = None
+
+            if live(i + LOAD):
+                load(i + LOAD)
+            if g_message is not None:
+                message(g_message)
+            if live(i + QUANTISE):
+                quantise_chunk(i + QUANTISE)
+            if live(i + NORMALISE):
+                normalise(i + NORMALISE)
+            if live(i + MULTIPLY):
+                multiply(i + MULTIPLY)
+            if g_stats is not None:
+                node_moments(g_stats)
+            if i == -1:
+                late["wv"] = weight_operand("wv", wv_rows, nc.vector.tensor_copy)
+            if i == U_ROUNDS[-1] + 1:
+                late["wu"] = weight_operand("wu", wu_rows, nc.vector.tensor_copy)
+            if live(i + TURN):
+                turn_chunk(i + TURN)
+            if g_out is not None:
+                square_of_mean(("node", g_out), 1)
+            if live(i + WEIGH):
+                weigh(i + WEIGH)
+            if g_out is not None:
+                inverse_std(("node", g_out), 1)
+            if live(i + SUM):
+                sum_over_j(i + SUM)
+            if live(i + MULTIPLY):
+                mean_over_graphs(i + MULTIPLY, CHUNKS[i + MULTIPLY][2])
+            if g_stats is not None:
+                mean_over_graphs(("node", g_stats), 1)
+            if live(i + TURN):
+                regroup_chunk(i + TURN, nc.scalar.copy if i + MULTIPLY < 0 else nc.vector.tensor_copy)
+            if live(i + NORMALISE):
+                add_residual(i + NORMALISE)
+            if g_out is not None:
+                shift = node_residual(g_out)
+            if live(i + MULTIPLY):
+                means_to_sbuf(i + MULTIPLY, CHUNKS[i + MULTIPLY][2])
+            if g_stats is not None:
+                means_to_sbuf(("node", g_stats), 1)
+            if i in U_ROUNDS:
+                make_u(i - U_ROUNDS[0])
+            if live(i + GATE):
+                gates(i + GATE)
+            if g_out is not None:
+                node_out(g_out, shift)

@@ -22,9 +22,7 @@ Q = C // P
 
 
 def chunk_list():
-    chunks = [(g, j0, CHUNK) for g in range(HALF) for j0 in range(0, N, CHUNK)]
-    g, j0, n = chunks[-1]
-    return chunks[:-1] + [(g, j0, n // 2), (g, j0 + n // 2, n // 4), (g, j0 + 3 * n // 4, n // 4)]
+    return [(g, j0, CHUNK) for g in range(HALF) for j0 in range(0, N, CHUNK)]
 
 
 CHUNKS = chunk_list()
@@ -65,6 +63,7 @@ def tile_graphmodel_pa_kernel(tc, x, edge, WA, WB, WE, WU, WV, out_0, out_1):
         codes_pool = ctx.enter_context(tc.tile_pool(name="codes", bufs=3))
         eo_pool = ctx.enter_context(tc.tile_pool(name="eo", bufs=4))
         junk_pool = ctx.enter_context(tc.tile_pool(name="junk", bufs=4))
+        gate_pool = ctx.enter_context(tc.tile_pool(name="gate", bufs=3))
         node_pool = ctx.enter_context(tc.tile_pool(name="node", bufs=2))
         small = ctx.enter_context(tc.tile_pool(name="small", bufs=4))
         work_ps = ctx.enter_context(tc.psum_pool(name="work_ps", bufs=3))
@@ -143,12 +142,14 @@ def tile_graphmodel_pa_kernel(tc, x, edge, WA, WB, WE, WU, WV, out_0, out_1):
             rows[k] = rows_pool.tile([P, CHUNK * C], BF16, name="rows")
             nc.sync.dma_start(out=rows[k][:, : n * C], in_=edge_rows[:, tile_cols(g * N + j0, C, n)])
 
-        we_rows, wa_rows, wb_rows = load_weight(WE), load_weight(WA), load_weight(WB)
+        we_rows = load_weight(WE)
         x_own = keep.tile([P, HALF * C], BF16)
         nc.sync.dma_start(out=x_own[:], in_=x_rows)
+        wa_rows = load_weight(WA)
         load(0)
-        wv_rows = load_weight(WV)
+        wb_rows = load_weight(WB)
         load(1)
+        wv_rows = load_weight(WV)
         wu_rows = load_weight(WU)
 
         def weight_operand(name, w_rows, copy):
@@ -160,32 +161,34 @@ def tile_graphmodel_pa_kernel(tc, x, edge, WA, WB, WE, WU, WV, out_0, out_1):
             return operand
 
         we = weight_operand("we", we_rows, nc.scalar.copy)
-        wa = weight_operand("wa", wa_rows, nc.scalar.copy)
-        wb = weight_operand("wb", wb_rows, nc.scalar.copy)
 
         xi = mx_operand(keep, "xi", HALF)
         xj = mx_operand(keep, "xj", N)
-        with tc.tile_pool(name="x_stage", bufs=1) as x_stage:
-            xi_grouped = x_stage.tile([P, HALF * C], BF16, align_bytes=64)
-            xj_grouped = x_stage.tile([P, N * C], BF16, align_bytes=64)
-            for turned_bank in turn(x_own[:].bitcast(F32), HALF):
-                regroup(nc.scalar.copy, turned_bank, xi_grouped[:].bitcast(F32))
-                bank, first, m = turned_bank
-                for a in range(m):
-                    by_half = bank[:, a, :, :].rearrange("p u (b h) -> p h b u", h=2)
-                    for h, copy in enumerate((nc.scalar.copy, nc.vector.tensor_copy)):
-                        copy(
-                            out=xj_grouped[:].bitcast(F32)[
-                                :, tile_cols(HALF * h + first + a, 2 * P)
-                            ].rearrange("p (b d u) -> p b d u", d=2, u=2),
-                            in_=by_half[:, h, :, :].unsqueeze(2).to_broadcast([P, B, 2, 2]),
-                        )
-            quantise(xi_grouped[:, : 4 * C], xi, slice(0, 4 * P))
-            quantise(xi_grouped[:, 4 * C :], xi, slice(4 * P, HALF * P))
-            for part in range(N // CHUNK):
-                quantise(xj_grouped[:, tile_cols(part, CHUNK * C)], xj, tile_cols(part, CHUNK * P))
+        xi_grouped = keep.tile([P, HALF * C], BF16, align_bytes=64)
+        xj_grouped = keep.tile([P, N * C], BF16, align_bytes=64)
 
-        gate_pool = ctx.enter_context(tc.tile_pool(name="gate", bufs=3))
+        def double_columns(j0, n):
+            h, g0 = divmod(j0, HALF)
+            source = xi_grouped[:].bitcast(F32)[:, tile_cols(g0, WORDS, n)].rearrange(
+                "p (m h u) -> p m h u", h=2, u=2
+            )[:, :, h, :]
+            nc.vector.tensor_copy(
+                out=xj_grouped[:].bitcast(F32)[:, tile_cols(j0, WORDS, n)].rearrange(
+                    "p (m d u) -> p m d u", d=2, u=2
+                ),
+                in_=source.unsqueeze(2).to_broadcast([P, n * B, 2, 2]),
+            )
+
+        def quantise_xj(part):
+            quantise(xj_grouped[:, tile_cols(part, CHUNK * C)], xj, tile_cols(part, CHUNK * P))
+
+        for turned_bank in turn(x_own[:].bitcast(F32), HALF):
+            regroup(nc.scalar.copy, turned_bank, xi_grouped[:].bitcast(F32))
+        double_columns(0, CHUNK)
+        quantise(xi_grouped[:, : 4 * C], xi, slice(0, 4 * P))
+        quantise_xj(0)
+        wa = weight_operand("wa", wa_rows, nc.scalar.copy)
+
 
         u_all = keep.tile([P, N * C], F32)
         late = {}
@@ -297,18 +300,20 @@ def tile_graphmodel_pa_kernel(tc, x, edge, WA, WB, WE, WU, WV, out_0, out_1):
             for cols in (tile_cols(0, half), tile_cols(1, half)):
                 nc.scalar.activation(out=gate[k][:, 0, cols], in_=gate[k][:, 0, cols], func=ACT.Exp, scale=0.5)
 
-        def weigh(k):
-            g, j0, n = CHUNKS[k]
-            nc.vector.tensor_mul(
-                out=gate[k][:, 1, : n * C], in0=gate[k][:, 0, : n * C], in1=u_all[:, tile_cols(j0, C, n)]
+        def weigh(engine, k, t0, n):
+            cols = tile_cols(t0, C, n)
+            engine.tensor_tensor(
+                out=gate[k][:, 1, cols], in0=gate[k][:, 0, cols],
+                in1=u_all[:, tile_cols(CHUNKS[k][1] + t0, C, n)], op=ALU.mult,
             )
 
-        def sum_over_j(k):
+        def sum_over_j(k, which=(0, 1)):
             g, j0, n = CHUNKS[k]
             if j0 == 0:
                 den_t[g] = sums_ps.tile([P, Q, P], F32, name="den_t")
                 num_t[g] = sums_ps.tile([P, Q, P], F32, name="num_t")
-            for s, total_t in enumerate((den_t[g], num_t[g])):
+            for s in which:
+                total_t = (den_t[g], num_t[g])[s]
                 for t in range(n):
                     for q in range(Q):
                         nc.tensor.matmul(
@@ -362,10 +367,41 @@ def tile_graphmodel_pa_kernel(tc, x, edge, WA, WB, WE, WU, WV, out_0, out_1):
 
         def node_out(g, shift):
             xo = node_pool.tile([P, C], F32, name="xo")
-            nc.scalar.activation(out=xo[:], in_=xn[g][:], func=ACT.Relu, bias=shift[:, 0:1], scale=1.0)
+            if g == HALF - 1:
+                nc.scalar.activation(out=xo[:], in_=xn[g][:], func=ACT.Relu, bias=shift[:, 0:1], scale=1.0)
+            else:
+                nc.gpsimd.tensor_scalar(
+                    out=xo[:], in0=xn[g][:], scalar1=shift[:, 0:1], scalar2=0.0, op0=ALU.add, op1=ALU.max
+                )
             nc.sync.dma_start(out=x_out_rows[:, tile_cols(g, C)], in_=xo[:])
 
-        for i in range(-TURN, len(CHUNKS) - NODE_OUT):
+        kept, uix_sb = {}, {}
+
+        def node_sums_out(g):
+            for s, total_t in enumerate((den_t[g], num_t[g])):
+                kept[g, s] = node_pool.tile([P, Q, P], F32, name=("rden_t", "msg_t")[s])
+                nc.vector.tensor_copy(out=kept[g, s][:], in_=total_t[:])
+
+        def node_uix(g):
+            uix_sb[g] = agg_ps.tile([P, Q, P], F32, name="uix_t", tag="agg")
+            for q in range(Q):
+                mx_pass(uix_sb[g][:, q, :], late["wu"], tile_cols(q), xi, tile_cols(g), True, True)
+            xn_t[g] = node_pool.tile([P, Q, P], F32, name="xn_t")
+
+        def node_recip(g, q, den, rden):
+            nc.vector.reciprocal(out=rden[:, q, :], in_=den[:, q, :])
+
+        def node_msg(g, q, num, rden):
+            nc.vector.tensor_mul(out=rden[:, q, :], in0=num[:, q, :], in1=rden[:, q, :])
+
+        def node_add(g, q, rden):
+            nc.vector.scalar_tensor_tensor(
+                out=xn_t[g][:, q, :], in0=rden[:, q, :], scalar=1.0 / N, in1=uix_sb[g][:, q, :],
+                op0=ALU.mult, op1=ALU.add,
+            )
+
+        last = len(CHUNKS) - 1
+        for i in range(-TURN, last):
             g_message = node_closed_by(i + MESSAGE)
             g_stats = node_closed_by(i + NODE_STATS)
             g_out = node_closed_by(i + NODE_OUT)
@@ -373,6 +409,8 @@ def tile_graphmodel_pa_kernel(tc, x, edge, WA, WB, WE, WU, WV, out_0, out_1):
 
             if live(i + LOAD):
                 load(i + LOAD)
+            if i == -TURN + 1:
+                wb = weight_operand("wb", wb_rows, nc.scalar.copy)
             if g_message is not None:
                 message(g_message)
             if live(i + QUANTISE):
@@ -383,6 +421,13 @@ def tile_graphmodel_pa_kernel(tc, x, edge, WA, WB, WE, WU, WV, out_0, out_1):
                 multiply(i + MULTIPLY)
             if g_stats is not None:
                 node_moments(g_stats)
+            if i == -TURN + 1:
+                double_columns(CHUNK, 2)
+                double_columns(CHUNK + 2, 2)
+                quantise(xi_grouped[:, 4 * C :], xi, slice(4 * P, HALF * P))
+                quantise_xj(1)
+                double_columns(2 * CHUNK, CHUNK)
+                quantise_xj(2)
             if i == -1:
                 late["wv"] = weight_operand("wv", wv_rows, nc.vector.tensor_copy)
             if i == U_ROUNDS[-1] + 1:
@@ -392,7 +437,7 @@ def tile_graphmodel_pa_kernel(tc, x, edge, WA, WB, WE, WU, WV, out_0, out_1):
             if g_out is not None:
                 square_of_mean(("node", g_out), 1)
             if live(i + WEIGH):
-                weigh(i + WEIGH)
+                weigh(nc.vector, i + WEIGH, 0, CHUNK)
             if g_out is not None:
                 inverse_std(("node", g_out), 1)
             if live(i + SUM):
@@ -417,3 +462,69 @@ def tile_graphmodel_pa_kernel(tc, x, edge, WA, WB, WE, WU, WV, out_0, out_1):
                 gates(i + GATE)
             if g_out is not None:
                 node_out(g_out, shift)
+
+        closing, before = HALF - 1, HALF - 2
+        key3 = ("node", before - 1)
+        sum_over_j(last - 3)
+        gates(last - 1)
+        square_of_mean(last, CHUNK)
+        for t in range(CHUNK):
+            relu_centred(last, t)
+        inverse_std(last, CHUNK)
+        square_of_mean(key3, 1)
+        node_sums_out(before)
+        add_residual(last)
+        gates(last)
+        inverse_std(key3, 1)
+        weigh(nc.vector, last - 2, 0, CHUNK)
+        sum_over_j(last - 2)
+        shift3 = node_residual(before - 1)
+        node_out(before - 1, shift3)
+        weigh(nc.vector, last - 1, 0, CHUNK)
+        node_uix(before)
+        node_uix(closing)
+        sum_over_j(last - 1)
+        weigh(nc.vector, last, 0, 2)
+        weigh(nc.vector, last, 2, 1)
+        weigh(nc.gpsimd, last, 3, 1)
+        sum_over_j(last, (0,))
+        sum_over_j(last, (1,))
+        for q in range(2):
+            node_recip(before, q, kept[before, 0], kept[before, 0])
+        rden = node_pool.tile([P, Q, P], F32, name="rden_t")
+        xn_ps = work_ps.tile([P, C], F32, name="xn_ps", tag="work")
+        for q in range(Q):
+            node_recip(closing, q, den_t[closing], rden)
+            if q > 0:
+                node_msg(closing, q - 1, num_t[closing], rden)
+            if q > 1:
+                node_add(closing, q - 2, rden)
+                nc.tensor.transpose(xn_ps[:, tile_cols(q - 2)], xn_t[closing][:, q - 2, :], ident[:])
+        node_msg(closing, Q - 1, num_t[closing], rden)
+        for q in (Q - 2, Q - 1):
+            node_add(closing, q, rden)
+            nc.tensor.transpose(xn_ps[:, tile_cols(q)], xn_t[closing][:, q, :], ident[:])
+        sums["node", closing] = small.tile([P, 2, 1], F32, name="sums")
+        xn[closing] = node_pool.tile([P, C], F32, name="xn")
+        moments(xn_ps[:], xn[closing][:], ("node", closing), 0)
+        for q in (2, 3):
+            node_recip(before, q, kept[before, 0], kept[before, 0])
+        mean_over_graphs(("node", closing), 1)
+        for q in range(2):
+            node_msg(before, q, kept[before, 1], kept[before, 0])
+        means_to_sbuf(("node", closing), 1)
+        node_msg(before, 2, kept[before, 1], kept[before, 0])
+        square_of_mean(("node", closing), 1)
+        node_msg(before, 3, kept[before, 1], kept[before, 0])
+        inverse_std(("node", closing), 1)
+        for q in range(Q):
+            node_add(before, q, kept[before, 0])
+        node_moments(before)
+        shift_last = node_residual(closing)
+        node_out(closing, shift_last)
+        mean_over_graphs(("node", before), 1)
+        means_to_sbuf(("node", before), 1)
+        square_of_mean(("node", before), 1)
+        inverse_std(("node", before), 1)
+        shift_last = node_residual(before)
+        node_out(before, shift_last)

@@ -31,6 +31,9 @@ LOAD, TURN, QUANTISE, MULTIPLY, NORMALISE, GATE, WEIGH, SUM = 5, 3, 2, 1, 0, -1,
 MESSAGE, NODE_STATS, NODE_OUT = -4, -5, -6
 U_ROUNDS = range(-WEIGH - 1, -WEIGH - 1 + N // CHUNK)
 
+PLAN = "||t0 t1|d n"
+PLANN = "|||t0 t1 d n"
+FIRST = True
 FLOPS = 2 * (B * N * N + 4 * B * N) * C * C
 
 
@@ -82,7 +85,7 @@ def tile_graphmodel_pa_kernel(tc, x, edge, WA, WB, WE, WU, WV, out_0, out_1):
             in0=parity[:].unsqueeze(1).to_broadcast([P, B, 2]),
             scalar1=1.0 / (B * C),
         )
-        minus_half = keep.tile([P, CHUNK], F32)
+        minus_half = keep.tile([P, CHUNK + 1], F32)
         nc.vector.memset(minus_half[:], -0.5)
 
         def turn(words, n):
@@ -242,8 +245,11 @@ def tile_graphmodel_pa_kernel(tc, x, edge, WA, WB, WE, WU, WV, out_0, out_1):
         turned, grouped_of, codes_of, eo, gate = {}, {}, {}, {}, {}
         den_t, num_t = {}, {}
 
-        def turn_chunk(k):
-            turned[k] = turn(rows[k][:].bitcast(F32), CHUNKS[k][2])
+        def turn_half(k, half):
+            bank, first, m = turn(rows[k][:, tile_cols(half, 2 * C)].bitcast(F32), 2)[0]
+            turned.setdefault(k, []).append((bank, 2 * half, 2))
+
+        def open_grouped(k):
             grouped_of[k] = grouped_pool.tile([P, CHUNK * C], BF16, align_bytes=64, name="grouped")
 
         def regroup_chunk(k, copy):
@@ -255,16 +261,23 @@ def tile_graphmodel_pa_kernel(tc, x, edge, WA, WB, WE, WU, WV, out_0, out_1):
             codes_of[k] = mx_operand(codes_pool, "edge", CHUNK)
             quantise(grouped_of[k][:, : n * C], codes_of[k], slice(0, n * P))
 
-        def multiply(k):
+        width = {}
+
+        def open_sums(k, n):
+            width[k] = n
+            sums[k] = small.tile([P, 2, n], F32, name="sums")
+
+        def multiply(k, pieces=((), (), (), ())):
             g, j0, n = CHUNKS[k]
             eo[k] = eo_pool.tile([P, CHUNK * C], F32, name="eo")
-            sums[k] = small.tile([P, 2, n], F32, name="sums")
             for t in range(n):
                 acc = agg_ps.tile([P, C], F32, name="acc", tag="agg")
                 mx_pass(acc[:], codes_of[k], tile_cols(t), we, slice(0, C), True, False)
                 mx_pass(acc[:], xi, tile_cols(g), wa, slice(0, C), False, False)
                 mx_pass(acc[:], xj, tile_cols(j0 + t), wb, slice(0, C), False, True)
                 moments(acc[:], eo[k][:, tile_cols(t, C)], k, t)
+                for piece in pieces[t]:
+                    piece()
 
         def relu_centred(k, t):
             nc.vector.tensor_scalar(
@@ -274,9 +287,9 @@ def tile_graphmodel_pa_kernel(tc, x, edge, WA, WB, WE, WU, WV, out_0, out_1):
 
         def normalise(k):
             n = CHUNKS[k][2]
-            square_of_mean(k, n)
+            square_of_mean(k, width[k])
             relu_centred(k, 0)
-            inverse_std(k, n)
+            inverse_std(k, width[k])
             for t in range(1, n):
                 relu_centred(k, t)
 
@@ -309,7 +322,7 @@ def tile_graphmodel_pa_kernel(tc, x, edge, WA, WB, WE, WU, WV, out_0, out_1):
 
         def sum_over_j(k, which=(0, 1)):
             g, j0, n = CHUNKS[k]
-            if j0 == 0:
+            if j0 == 0 and which[0] == 0:
                 den_t[g] = sums_ps.tile([P, Q, P], F32, name="den_t")
                 num_t[g] = sums_ps.tile([P, Q, P], F32, name="num_t")
             for s in which:
@@ -345,22 +358,25 @@ def tile_graphmodel_pa_kernel(tc, x, edge, WA, WB, WE, WU, WV, out_0, out_1):
                     op0=ALU.mult, op1=ALU.add,
                 )
 
-        def node_moments(g):
+        where = {}
+
+        def node_moments(g, key, col):
             xn_ps = work_ps.tile([P, C], F32, name="xn_ps", tag="work")
             for q in range(Q):
                 nc.tensor.transpose(xn_ps[:, tile_cols(q)], xn_t[g][:, q, :], ident[:])
-            sums["node", g] = small.tile([P, 2, 1], F32, name="sums")
             xn[g] = node_pool.tile([P, C], F32, name="xn")
-            moments(xn_ps[:], xn[g][:], ("node", g), 0)
+            where[g] = key, col
+            moments(xn_ps[:], xn[g][:], key, col)
 
         def node_residual(g):
+            key, col = where[g]
             shift = small.tile([P, 1], F32, name="shift")
             nc.vector.scalar_tensor_tensor(
-                out=shift[:], in0=avg["node", g][:, 0, :], scalar=-1.0, in1=rstd["node", g][:],
+                out=shift[:], in0=avg[key][:, 0, col : col + 1], scalar=-1.0, in1=rstd[key][:, col : col + 1],
                 op0=ALU.mult, op1=ALU.mult,
             )
             nc.vector.scalar_tensor_tensor(
-                out=xn[g][:], in0=xn[g][:], scalar=rstd["node", g][:, 0:1],
+                out=xn[g][:], in0=xn[g][:], scalar=rstd[key][:, col : col + 1],
                 in1=x_own[:, tile_cols(g, C)], op0=ALU.mult, op1=ALU.add,
             )
             return shift
@@ -418,9 +434,31 @@ def tile_graphmodel_pa_kernel(tc, x, edge, WA, WB, WE, WU, WV, out_0, out_1):
             if live(i + NORMALISE):
                 normalise(i + NORMALISE)
             if live(i + MULTIPLY):
-                multiply(i + MULTIPLY)
-            if g_stats is not None:
-                node_moments(g_stats)
+                open_sums(i + MULTIPLY, CHUNK + (g_stats is not None))
+            if g_stats is not None and FIRST:
+                node_moments(g_stats, i + MULTIPLY, CHUNK)
+            if i == -1:
+                late["wv"] = weight_operand("wv", wv_rows, nc.vector.tensor_copy)
+            if i == U_ROUNDS[-1] + 1:
+                late["wu"] = weight_operand("wu", wu_rows, nc.vector.tensor_copy)
+            ks, kt = i + SUM, i + TURN
+            pieces = {}
+            if live(kt):
+                pieces["t0"] = lambda: turn_half(kt, 0)
+                pieces["t1"] = lambda: turn_half(kt, 1)
+            if live(ks):
+                pieces["d"] = lambda: sum_over_j(ks, (0,))
+                pieces["n"] = lambda: sum_over_j(ks, (1,))
+            plan = (PLANN if g_message is not None else PLAN).split("|")
+            plan = [[pieces[x] for x in o.split() if x in pieces] for o in plan]
+            if live(i + MULTIPLY):
+                multiply(i + MULTIPLY, plan)
+            else:
+                for o in plan:
+                    for x in o:
+                        x()
+            if g_stats is not None and not FIRST:
+                node_moments(g_stats, i + MULTIPLY, CHUNK)
             if i == -TURN + 1:
                 double_columns(CHUNK, 2)
                 double_columns(CHUNK + 2, 2)
@@ -428,24 +466,12 @@ def tile_graphmodel_pa_kernel(tc, x, edge, WA, WB, WE, WU, WV, out_0, out_1):
                 quantise_xj(1)
                 double_columns(2 * CHUNK, CHUNK)
                 quantise_xj(2)
-            if i == -1:
-                late["wv"] = weight_operand("wv", wv_rows, nc.vector.tensor_copy)
-            if i == U_ROUNDS[-1] + 1:
-                late["wu"] = weight_operand("wu", wu_rows, nc.vector.tensor_copy)
             if live(i + TURN):
-                turn_chunk(i + TURN)
-            if g_out is not None:
-                square_of_mean(("node", g_out), 1)
+                open_grouped(i + TURN)
             if live(i + WEIGH):
                 weigh(nc.vector, i + WEIGH, 0, CHUNK)
-            if g_out is not None:
-                inverse_std(("node", g_out), 1)
-            if live(i + SUM):
-                sum_over_j(i + SUM)
             if live(i + MULTIPLY):
-                mean_over_graphs(i + MULTIPLY, CHUNKS[i + MULTIPLY][2])
-            if g_stats is not None:
-                mean_over_graphs(("node", g_stats), 1)
+                mean_over_graphs(i + MULTIPLY, width[i + MULTIPLY])
             if live(i + TURN):
                 regroup_chunk(i + TURN, nc.scalar.copy if i + MULTIPLY < 0 else nc.vector.tensor_copy)
             if live(i + NORMALISE):
@@ -453,9 +479,7 @@ def tile_graphmodel_pa_kernel(tc, x, edge, WA, WB, WE, WU, WV, out_0, out_1):
             if g_out is not None:
                 shift = node_residual(g_out)
             if live(i + MULTIPLY):
-                means_to_sbuf(i + MULTIPLY, CHUNKS[i + MULTIPLY][2])
-            if g_stats is not None:
-                means_to_sbuf(("node", g_stats), 1)
+                means_to_sbuf(i + MULTIPLY, width[i + MULTIPLY])
             if i in U_ROUNDS:
                 make_u(i - U_ROUNDS[0])
             if live(i + GATE):
@@ -464,18 +488,15 @@ def tile_graphmodel_pa_kernel(tc, x, edge, WA, WB, WE, WU, WV, out_0, out_1):
                 node_out(g_out, shift)
 
         closing, before = HALF - 1, HALF - 2
-        key3 = ("node", before - 1)
         sum_over_j(last - 3)
         gates(last - 1)
-        square_of_mean(last, CHUNK)
+        square_of_mean(last, width[last])
         for t in range(CHUNK):
             relu_centred(last, t)
-        inverse_std(last, CHUNK)
-        square_of_mean(key3, 1)
+        inverse_std(last, width[last])
         node_sums_out(before)
         add_residual(last)
         gates(last)
-        inverse_std(key3, 1)
         weigh(nc.vector, last - 2, 0, CHUNK)
         sum_over_j(last - 2)
         shift3 = node_residual(before - 1)
@@ -504,27 +525,29 @@ def tile_graphmodel_pa_kernel(tc, x, edge, WA, WB, WE, WU, WV, out_0, out_1):
         for q in (Q - 2, Q - 1):
             node_add(closing, q, rden)
             nc.tensor.transpose(xn_ps[:, tile_cols(q)], xn_t[closing][:, q, :], ident[:])
-        sums["node", closing] = small.tile([P, 2, 1], F32, name="sums")
+        open_sums("closing", 1)
         xn[closing] = node_pool.tile([P, C], F32, name="xn")
-        moments(xn_ps[:], xn[closing][:], ("node", closing), 0)
+        where[closing] = "closing", 0
+        moments(xn_ps[:], xn[closing][:], "closing", 0)
         for q in (2, 3):
             node_recip(before, q, kept[before, 0], kept[before, 0])
-        mean_over_graphs(("node", closing), 1)
+        mean_over_graphs("closing", 1)
         for q in range(2):
             node_msg(before, q, kept[before, 1], kept[before, 0])
-        means_to_sbuf(("node", closing), 1)
+        means_to_sbuf("closing", 1)
         node_msg(before, 2, kept[before, 1], kept[before, 0])
-        square_of_mean(("node", closing), 1)
+        square_of_mean("closing", 1)
         node_msg(before, 3, kept[before, 1], kept[before, 0])
-        inverse_std(("node", closing), 1)
+        inverse_std("closing", 1)
         for q in range(Q):
             node_add(before, q, kept[before, 0])
-        node_moments(before)
+        open_sums("before", 1)
+        node_moments(before, "before", 0)
         shift_last = node_residual(closing)
         node_out(closing, shift_last)
-        mean_over_graphs(("node", before), 1)
-        means_to_sbuf(("node", before), 1)
-        square_of_mean(("node", before), 1)
-        inverse_std(("node", before), 1)
+        mean_over_graphs("before", 1)
+        means_to_sbuf("before", 1)
+        square_of_mean("before", 1)
+        inverse_std("before", 1)
         shift_last = node_residual(before)
         node_out(before, shift_last)

@@ -290,7 +290,9 @@ def tile_graphmodel_pa_kernel(tc, x, edge, WA, WB, WE, WU, WV, out_0, out_1):
             square_of_mean(k, width[k])
             relu_centred(k, 0)
             inverse_std(k, width[k])
-            for t in range(1, n):
+
+        def normalise_rest(k):
+            for t in range(1, CHUNKS[k][2]):
                 relu_centred(k, t)
 
         def add_residual(k):
@@ -427,20 +429,25 @@ def tile_graphmodel_pa_kernel(tc, x, edge, WA, WB, WE, WU, WV, out_0, out_1):
                 load(i + LOAD)
             if i == -TURN + 1:
                 wb = weight_operand("wb", wb_rows, nc.scalar.copy)
+            early = g_message is not None and not live(i + TURN)
+            if early and live(i):
+                normalise(i)
             if g_message is not None:
                 message(g_message)
             if live(i + QUANTISE):
                 quantise_chunk(i + QUANTISE)
             if live(i + NORMALISE):
-                normalise(i + NORMALISE)
+                if not early:
+                    normalise(i + NORMALISE)
+                normalise_rest(i + NORMALISE)
             if live(i + MULTIPLY):
                 open_sums(i + MULTIPLY, CHUNK + (g_stats is not None))
             if g_stats is not None and FIRST:
                 node_moments(g_stats, i + MULTIPLY, CHUNK)
             if i == -1:
-                late["wv"] = weight_operand("wv", wv_rows, nc.vector.tensor_copy)
+                late["wv"] = weight_operand("wv", wv_rows, nc.scalar.copy)
             if i == U_ROUNDS[-1] + 1:
-                late["wu"] = weight_operand("wu", wu_rows, nc.vector.tensor_copy)
+                late["wu"] = weight_operand("wu", wu_rows, nc.scalar.copy)
             ks, kt = i + SUM, i + TURN
             pieces = {}
             if live(kt):
@@ -506,8 +513,7 @@ def tile_graphmodel_pa_kernel(tc, x, edge, WA, WB, WE, WU, WV, out_0, out_1):
         node_uix(closing)
         sum_over_j(last - 1)
         weigh(nc.vector, last, 0, 2)
-        weigh(nc.vector, last, 2, 1)
-        weigh(nc.gpsimd, last, 3, 1)
+        weigh(nc.vector, last, 2, 2)
         sum_over_j(last, (0,))
         sum_over_j(last, (1,))
         for q in range(2):

@@ -34,6 +34,8 @@ U_ROUNDS = range(-WEIGH - 1, -WEIGH - 1 + N // CHUNK)
 PLAN = "||t0 t1|d n"
 PLANN = "|||t0 t1 d n"
 FIRST = True
+MODE = 1
+LATE = lambda k: k > 5
 FLOPS = 2 * (B * N * N + 4 * B * N) * C * C
 
 
@@ -205,9 +207,15 @@ def tile_graphmodel_pa_kernel(tc, x, edge, WA, WB, WE, WU, WV, out_0, out_1):
         sums, total, avg, mean_sq, rstd = {}, {}, {}, {}, {}
 
         def moments(src, dst, key, col):
+            first_moment(src, dst, key, col)
+            second_moment(src, key, col)
+
+        def first_moment(src, dst, key, col):
             nc.scalar.activation(
                 out=dst, in_=src, func=ACT.Identity, accum_out=sums[key][:, 0, col : col + 1]
             )
+
+        def second_moment(src, key, col):
             junk = junk_pool.tile([P, C], BF16, name="junk")
             nc.scalar.activation(
                 out=junk[:], in_=src, func=ACT.Square, accum_out=sums[key][:, 1, col : col + 1]
@@ -275,9 +283,15 @@ def tile_graphmodel_pa_kernel(tc, x, edge, WA, WB, WE, WU, WV, out_0, out_1):
                 mx_pass(acc[:], codes_of[k], tile_cols(t), we, slice(0, C), True, False)
                 mx_pass(acc[:], xi, tile_cols(g), wa, slice(0, C), False, False)
                 mx_pass(acc[:], xj, tile_cols(j0 + t), wb, slice(0, C), False, True)
-                moments(acc[:], eo[k][:, tile_cols(t, C)], k, t)
+                first_moment(acc[:], eo[k][:, tile_cols(t, C)], k, t)
                 for piece in pieces[t]:
                     piece()
+                if not LATE(k):
+                    second_moment(acc[:], k, t)
+                elif t >= 1:
+                    second_moment(eo[k][:, tile_cols(t - 1, C)], k, t - 1)
+            if LATE(k):
+                second_moment(eo[k][:, tile_cols(n - 1, C)], k, n - 1)
 
         def relu_centred(k, t):
             nc.vector.tensor_scalar(
@@ -342,23 +356,20 @@ def tile_graphmodel_pa_kernel(tc, x, edge, WA, WB, WE, WU, WV, out_0, out_1):
 
         xn_t, xn = {}, {}
 
-        def message(g):
+        def message(g, then):
             uix_t = work_ps.tile([P, Q, P], F32, name="uix_t", tag="work")
             for q in range(Q):
                 mx_pass(uix_t[:, q, :], late["wu"], tile_cols(q), xi, tile_cols(g), True, True)
             rden_t = node_pool.tile([P, Q, P], F32, name="rden_t")
             msg_t = node_pool.tile([P, Q, P], F32, name="msg_t")
             xn_t[g] = node_pool.tile([P, Q, P], F32, name="xn_t")
-            halves = (slice(0, Q // 2), slice(Q // 2, Q))
-            for qs in halves:
-                nc.vector.reciprocal(out=rden_t[:, qs, :], in_=den_t[g][:, qs, :])
-            for qs in halves:
-                nc.vector.tensor_mul(out=msg_t[:, qs, :], in0=num_t[g][:, qs, :], in1=rden_t[:, qs, :])
-            for qs in halves:
-                nc.vector.scalar_tensor_tensor(
-                    out=xn_t[g][:, qs, :], in0=msg_t[:, qs, :], scalar=1.0 / N, in1=uix_t[:, qs, :],
-                    op0=ALU.mult, op1=ALU.add,
-                )
+            nc.vector.reciprocal(out=rden_t[:], in_=den_t[g][:])
+            then[0]()
+            nc.vector.tensor_mul(out=msg_t[:], in0=num_t[g][:], in1=rden_t[:])
+            then[1]()
+            nc.vector.scalar_tensor_tensor(
+                out=xn_t[g][:], in0=msg_t[:], scalar=1.0 / N, in1=uix_t[:], op0=ALU.mult, op1=ALU.add,
+            )
 
         where = {}
 
@@ -432,14 +443,23 @@ def tile_graphmodel_pa_kernel(tc, x, edge, WA, WB, WE, WU, WV, out_0, out_1):
             early = g_message is not None and not live(i + TURN)
             if early and live(i):
                 normalise(i)
+            def quantise_next():
+                if live(i + QUANTISE):
+                    quantise_chunk(i + QUANTISE)
+
+            def normalise_now():
+                if live(i) and not early:
+                    normalise(i)
+                if live(i):
+                    normalise_rest(i)
+
             if g_message is not None:
-                message(g_message)
-            if live(i + QUANTISE):
-                quantise_chunk(i + QUANTISE)
-            if live(i + NORMALISE):
-                if not early:
-                    normalise(i + NORMALISE)
-                normalise_rest(i + NORMALISE)
+                message(g_message, ((quantise_next, normalise_now), (quantise_next, lambda: None))[MODE])
+                if MODE == 1:
+                    normalise_now()
+            else:
+                quantise_next()
+                normalise_now()
             if live(i + MULTIPLY):
                 open_sums(i + MULTIPLY, CHUNK + (g_stats is not None))
             if g_stats is not None and FIRST:

@@ -239,16 +239,19 @@ def tile_graphmodel_pa_kernel(tc, x, edge, WA, WB, WE, WU, WV, out_0, out_1):
             mean_sq[key] = small.tile([P, n], F32, name="mean_sq")
             nc.vector.tensor_mul(out=mean_sq[key][:], in0=avg[key][:, 0, :], in1=avg[key][:, 0, :])
 
-        def inverse_std(key, n):
+        def inverse_std(key, n, on_scalar=False):
             var_eps = small.tile([P, n], F32, name="var_eps")
             nc.vector.scalar_tensor_tensor(
                 out=var_eps[:], in0=avg[key][:, 1, :], scalar=BN_EPS, in1=mean_sq[key][:],
                 op0=ALU.add, op1=ALU.subtract,
             )
             rstd[key] = small.tile([P, n], F32, name="rstd")
-            nc.gpsimd.tensor_tensor(
-                out=rstd[key][:], in0=var_eps[:], in1=minus_half[:, :n], op=ALU.pow
-            )
+            if on_scalar:
+                nc.scalar.activation(out=rstd[key][:], in_=var_eps[:], func=ACT.Abs_reciprocal_sqrt)
+            else:
+                nc.gpsimd.tensor_tensor(
+                    out=rstd[key][:], in0=var_eps[:], in1=minus_half[:, :n], op=ALU.pow
+                )
 
         turned, grouped_of, codes_of, eo, gate = {}, {}, {}, {}, {}
         den_t, num_t = {}, {}
@@ -396,7 +399,7 @@ def tile_graphmodel_pa_kernel(tc, x, edge, WA, WB, WE, WU, WV, out_0, out_1):
 
         def node_out(g, shift):
             xo = node_pool.tile([P, C], F32, name="xo")
-            if g == HALF - 1:
+            if g >= HALF - 2:
                 nc.scalar.activation(out=xo[:], in_=xn[g][:], func=ACT.Relu, bias=shift[:, 0:1], scale=1.0)
             else:
                 nc.gpsimd.tensor_scalar(
@@ -404,7 +407,7 @@ def tile_graphmodel_pa_kernel(tc, x, edge, WA, WB, WE, WU, WV, out_0, out_1):
                 )
             nc.sync.dma_start(out=x_out_rows[:, tile_cols(g, C)], in_=xo[:])
 
-        kept, uix_sb = {}, {}
+        kept, uix_ps, rden = {}, {}, {}
 
         def node_sums_out(g):
             for s, total_t in enumerate((den_t[g], num_t[g])):
@@ -412,20 +415,23 @@ def tile_graphmodel_pa_kernel(tc, x, edge, WA, WB, WE, WU, WV, out_0, out_1):
                 nc.vector.tensor_copy(out=kept[g, s][:], in_=total_t[:])
 
         def node_uix(g):
-            uix_sb[g] = agg_ps.tile([P, Q, P], F32, name="uix_t", tag="agg")
+            uix_ps[g] = agg_ps.tile([P, Q, P], F32, name="uix_t", tag="agg")
             for q in range(Q):
-                mx_pass(uix_sb[g][:, q, :], late["wu"], tile_cols(q), xi, tile_cols(g), True, True)
+                mx_pass(uix_ps[g][:, q, :], late["wu"], tile_cols(q), xi, tile_cols(g), True, True)
             xn_t[g] = node_pool.tile([P, Q, P], F32, name="xn_t")
 
-        def node_recip(g, q, den, rden):
-            nc.vector.reciprocal(out=rden[:, q, :], in_=den[:, q, :])
+        def inverse_root(g, den, qs):
+            nc.scalar.activation(out=rden[g][:, qs, :], in_=den[:, qs, :], func=ACT.Abs_reciprocal_sqrt)
 
-        def node_msg(g, q, num, rden):
-            nc.vector.tensor_mul(out=rden[:, q, :], in0=num[:, q, :], in1=rden[:, q, :])
+        def inverse(g, qs):
+            nc.scalar.activation(out=rden[g][:, qs, :], in_=rden[g][:, qs, :], func=ACT.Square)
 
-        def node_add(g, q, rden):
+        def node_msg(g, num, qs):
+            nc.vector.tensor_mul(out=rden[g][:, qs, :], in0=num[:, qs, :], in1=rden[g][:, qs, :])
+
+        def node_add(g, qs):
             nc.vector.scalar_tensor_tensor(
-                out=xn_t[g][:, q, :], in0=rden[:, q, :], scalar=1.0 / N, in1=uix_sb[g][:, q, :],
+                out=xn_t[g][:, qs, :], in0=rden[g][:, qs, :], scalar=1.0 / N, in1=uix_ps[g][:, qs, :],
                 op0=ALU.mult, op1=ALU.add,
             )
 
@@ -515,6 +521,7 @@ def tile_graphmodel_pa_kernel(tc, x, edge, WA, WB, WE, WU, WV, out_0, out_1):
                 node_out(g_out, shift)
 
         closing, before = HALF - 1, HALF - 2
+        every, halves = slice(0, Q), (slice(0, Q // 2), slice(Q // 2, Q))
         sum_over_j(last - 3)
         gates(last - 1)
         square_of_mean(last, width[last])
@@ -526,54 +533,39 @@ def tile_graphmodel_pa_kernel(tc, x, edge, WA, WB, WE, WU, WV, out_0, out_1):
         gates(last)
         weigh(nc.vector, last - 2, 0, CHUNK)
         sum_over_j(last - 2)
-        shift3 = node_residual(before - 1)
-        node_out(before - 1, shift3)
+        shift = node_residual(before - 1)
+        node_out(before - 1, shift)
         weigh(nc.vector, last - 1, 0, CHUNK)
         node_uix(before)
         node_uix(closing)
         sum_over_j(last - 1)
+        sum_over_j(last, (0,))
         weigh(nc.vector, last, 0, 2)
         weigh(nc.vector, last, 2, 2)
-        sum_over_j(last, (0,))
         sum_over_j(last, (1,))
-        for q in range(2):
-            node_recip(before, q, kept[before, 0], kept[before, 0])
-        rden = node_pool.tile([P, Q, P], F32, name="rden_t")
-        xn_ps = work_ps.tile([P, C], F32, name="xn_ps", tag="work")
-        for q in range(Q):
-            node_recip(closing, q, den_t[closing], rden)
-            if q > 0:
-                node_msg(closing, q - 1, num_t[closing], rden)
-            if q > 1:
-                node_add(closing, q - 2, rden)
-                nc.tensor.transpose(xn_ps[:, tile_cols(q - 2)], xn_t[closing][:, q - 2, :], ident[:])
-        node_msg(closing, Q - 1, num_t[closing], rden)
-        for q in (Q - 2, Q - 1):
-            node_add(closing, q, rden)
-            nc.tensor.transpose(xn_ps[:, tile_cols(q)], xn_t[closing][:, q, :], ident[:])
-        open_sums("closing", 1)
-        xn[closing] = node_pool.tile([P, C], F32, name="xn")
-        where[closing] = "closing", 0
-        moments(xn_ps[:], xn[closing][:], "closing", 0)
-        for q in (2, 3):
-            node_recip(before, q, kept[before, 0], kept[before, 0])
-        mean_over_graphs("closing", 1)
-        for q in range(2):
-            node_msg(before, q, kept[before, 1], kept[before, 0])
-        means_to_sbuf("closing", 1)
-        node_msg(before, 2, kept[before, 1], kept[before, 0])
-        square_of_mean("closing", 1)
-        node_msg(before, 3, kept[before, 1], kept[before, 0])
-        inverse_std("closing", 1)
-        for q in range(Q):
-            node_add(before, q, kept[before, 0])
+        rden[before] = kept[before, 0]
+        rden[closing] = node_pool.tile([P, Q, P], F32, name="rden_t")
+        inverse_root(before, kept[before, 0], every)
+        inverse(before, every)
+        node_msg(before, kept[before, 1], every)
+        for qs in halves:
+            inverse_root(closing, den_t[closing], qs)
+        node_add(before, every)
+        for qs in halves:
+            inverse(closing, qs)
         open_sums("before", 1)
+        open_sums("closing", 1)
+        for qs in halves:
+            node_msg(closing, num_t[closing], qs)
+        for qs in halves:
+            node_add(closing, qs)
         node_moments(before, "before", 0)
-        shift_last = node_residual(closing)
-        node_out(closing, shift_last)
-        mean_over_graphs("before", 1)
-        means_to_sbuf("before", 1)
-        square_of_mean("before", 1)
-        inverse_std("before", 1)
-        shift_last = node_residual(before)
-        node_out(before, shift_last)
+        node_moments(closing, "closing", 0)
+        for key in ("before", "closing"):
+            mean_over_graphs(key, 1)
+        for key, g in (("before", before), ("closing", closing)):
+            means_to_sbuf(key, 1)
+            square_of_mean(key, 1)
+            inverse_std(key, 1, on_scalar=True)
+            shift = node_residual(g)
+            node_out(g, shift)

from contextlib import ExitStack

import concourse.mybir as mybir
from concourse.masks import make_identity

F32 = mybir.dt.float32
BF16 = mybir.dt.bfloat16
U32 = mybir.dt.uint32
U8 = mybir.dt.uint8
FP8X4 = mybir.dt.float8_e4m3fn_x4
ALU = mybir.AluOpType
ACT = mybir.ActivationFunctionType
AX = mybir.AxisListType

B, N, C = 64, 12, 512
BN_EPS = 1e-5
P = 128
HALF = N // 2
CHUNK = 4
WORDS = C // 2
Q = C // P


def chunk_list():
    return [(g, j0, CHUNK) for g in range(HALF) for j0 in range(0, N, CHUNK)]


CHUNKS = chunk_list()

LOAD, TURN, QUANTISE, MULTIPLY, NORMALISE, GATE, WEIGH, SUM = 5, 3, 2, 1, 0, -1, -2, -3
MESSAGE, NODE_STATS, NODE_OUT = -4, -5, -6
U_ROUNDS = range(-WEIGH - 1, -WEIGH - 1 + N // CHUNK)

PLAN = "||t0 t1|d n"
PLANN = "|||t0 t1 d n"
FIRST = True
MODE = 1
LATE = lambda k: k > 5
FLOPS = 2 * (B * N * N + 4 * B * N) * C * C


def tile_cols(t, width=P, n=1):
    return slice(t * width, (t + n) * width)


def live(k):
    return 0 <= k < len(CHUNKS)


def node_closed_by(k):
    if live(k) and CHUNKS[k][1] + CHUNKS[k][2] == N:
        return CHUNKS[k][0]
    return None


def tile_graphmodel_pa_kernel(tc, x, edge, WA, WB, WE, WU, WV, out_0, out_1):
    nc = tc.nc
    edge_rows = edge.rearrange("b (h t) c -> (b h) (t c)", h=2)
    edge_out_rows = out_1.rearrange("b (h t) c -> (b h) (t c)", h=2)
    x_rows = x.rearrange("b (h g) c -> (b h) (g c)", h=2)
    x_out_rows = out_0.rearrange("b (h g) c -> (b h) (g c)", h=2)

    with ExitStack() as ctx:
        ctx.enter_context(tc.manual_schedule())
        keep = ctx.enter_context(tc.tile_pool(name="keep", bufs=1))
        rows_pool = ctx.enter_context(tc.tile_pool(name="rows", bufs=8))
        grouped_pool = ctx.enter_context(tc.tile_pool(name="grouped", bufs=3))
        codes_pool = ctx.enter_context(tc.tile_pool(name="codes", bufs=3))
        eo_pool = ctx.enter_context(tc.tile_pool(name="eo", bufs=4))
        junk_pool = ctx.enter_context(tc.tile_pool(name="junk", bufs=4))
        gate_pool = ctx.enter_context(tc.tile_pool(name="gate", bufs=3))
        node_pool = ctx.enter_context(tc.tile_pool(name="node", bufs=2))
        small = ctx.enter_context(tc.tile_pool(name="small", bufs=4))
        work_ps = ctx.enter_context(tc.psum_pool(name="work_ps", bufs=3))
        agg_ps = ctx.enter_context(tc.psum_pool(name="agg_ps", bufs=3))
        sums_ps = ctx.enter_context(tc.psum_pool(name="sums_ps", bufs=1))

        ident = keep.tile([P, P], F32)
        make_identity(nc, ident[:])
        parity = keep.tile([P, 2], F32)
        nc.vector.tensor_reduce(
            out=parity[:], in_=ident[:].rearrange("p (b h) -> p h b", h=2), axis=AX.X, op=ALU.add
        )
        same_half = keep.tile([P, P], F32)
        nc.vector.tensor_scalar_mul(
            out=same_half[:].rearrange("p (b h) -> p b h", h=2),
            in0=parity[:].unsqueeze(1).to_broadcast([P, B, 2]),
            scalar1=1.0 / (B * C),
        )
        minus_half = keep.tile([P, CHUNK + 1], F32)
        nc.vector.memset(minus_half[:], -0.5)

        def turn(words, n):
            banks = []
            for first in range(0, n, 2):
                m = min(2, n - first)
                bank = work_ps.tile([P, 2, 2, P], F32, name="turned", tag="work")
                for a in range(m):
                    for u in range(2):
                        start = (first + a) * WORDS
                        nc.tensor.transpose(bank[:, a, u, :], words[:, start + u : start + WORDS : 2], ident[:])
                banks.append((bank, first, m))
            return banks

        def regroup(copy, turned_bank, grouped_words):
            bank, first, m = turned_bank
            copy(
                out=grouped_words[:, tile_cols(first, 2 * P, m)].rearrange(
                    "p (a r u) -> p a r u", a=m, u=2
                ),
                in_=bank[:, :m, :, :].rearrange("p a u r -> p a r u"),
            )

        def quantise(grouped, operand, cols):
            nc.vector.quantize_mx(
                out=operand[0][:, cols].bitcast(FP8X4), scales=operand[1][:, cols], in_=grouped
            )

        def mx_operand(pool, name, n):
            codes = pool.tile([P, n * P], U32, align_bytes=64, name="codes_" + name)
            scales = pool.tile([P, n * P], U8, align_bytes=64, name="scales_" + name)
            return codes, scales

        def mx_pass(out, left, left_cols, right, right_cols, start, stop):
            nc.tensor.matmul_mx(
                out=out,
                lhsT=left[0][:, left_cols].bitcast(FP8X4),
                lhsT_scale=left[1][:, left_cols],
                rhs=right[0][:, right_cols].bitcast(FP8X4),
                rhs_scale=right[1][:, right_cols],
                start=start,
                stop=stop,
            )

        def load_weight(w):
            w_rows = rows_pool.tile([P, CHUNK * C], BF16, name="rows")
            nc.sync.dma_start(
                out=w_rows[:].rearrange("p (a k) -> p a k", a=Q),
                in_=w.rearrange("(a p) k -> p a k", p=P),
            )
            return w_rows

        rows = {}

        def load(k):
            g, j0, n = CHUNKS[k]
            rows[k] = rows_pool.tile([P, CHUNK * C], BF16, name="rows")
            nc.sync.dma_start(out=rows[k][:, : n * C], in_=edge_rows[:, tile_cols(g * N + j0, C, n)])

        we_rows = load_weight(WE)
        x_own = keep.tile([P, HALF * C], BF16)
        nc.sync.dma_start(out=x_own[:], in_=x_rows)
        wa_rows = load_weight(WA)
        load(0)
        wb_rows = load_weight(WB)
        load(1)
        wv_rows = load_weight(WV)
        wu_rows = load_weight(WU)

        def weight_operand(name, w_rows, copy):
            operand = mx_operand(keep, name, Q)
            grouped = grouped_pool.tile([P, CHUNK * C], BF16, align_bytes=64, name="grouped")
            for turned_bank in turn(w_rows[:].bitcast(F32), Q):
                regroup(copy, turned_bank, grouped[:].bitcast(F32))
            quantise(grouped[:], operand, slice(0, C))
            return operand

        we = weight_operand("we", we_rows, nc.scalar.copy)

        xi = mx_operand(keep, "xi", HALF)
        xj = mx_operand(keep, "xj", N)
        xi_grouped = keep.tile([P, HALF * C], BF16, align_bytes=64)
        xj_grouped = keep.tile([P, N * C], BF16, align_bytes=64)

        def double_columns(j0, n):
            h, g0 = divmod(j0, HALF)
            source = xi_grouped[:].bitcast(F32)[:, tile_cols(g0, WORDS, n)].rearrange(
                "p (m h u) -> p m h u", h=2, u=2
            )[:, :, h, :]
            nc.vector.tensor_copy(
                out=xj_grouped[:].bitcast(F32)[:, tile_cols(j0, WORDS, n)].rearrange(
                    "p (m d u) -> p m d u", d=2, u=2
                ),
                in_=source.unsqueeze(2).to_broadcast([P, n * B, 2, 2]),
            )

        def quantise_xj(part):
            quantise(xj_grouped[:, tile_cols(part, CHUNK * C)], xj, tile_cols(part, CHUNK * P))

        for turned_bank in turn(x_own[:].bitcast(F32), HALF):
            regroup(nc.scalar.copy, turned_bank, xi_grouped[:].bitcast(F32))
        double_columns(0, CHUNK)
        quantise(xi_grouped[:, : 4 * C], xi, slice(0, 4 * P))
        quantise_xj(0)
        wa = weight_operand("wa", wa_rows, nc.scalar.copy)


        u_all = keep.tile([P, N * C], F32)
        late = {}

        def make_u(part):
            for j in range(part * CHUNK, (part + 1) * CHUNK):
                acc = agg_ps.tile([P, C], F32, name="acc", tag="agg")
                mx_pass(acc[:], xj, tile_cols(j), late["wv"], slice(0, C), True, True)
                nc.vector.tensor_copy(out=u_all[:, tile_cols(j, C)], in_=acc[:])

        sums, total, avg, mean_sq, rstd = {}, {}, {}, {}, {}

        def moments(src, dst, key, col):
            first_moment(src, dst, key, col)
            second_moment(src, key, col)

        def first_moment(src, dst, key, col):
            nc.scalar.activation(
                out=dst, in_=src, func=ACT.Identity, accum_out=sums[key][:, 0, col : col + 1]
            )

        def second_moment(src, key, col):
            junk = junk_pool.tile([P, C], BF16, name="junk")
            nc.scalar.activation(
                out=junk[:], in_=src, func=ACT.Square, accum_out=sums[key][:, 1, col : col + 1]
            )

        def mean_over_graphs(key, n):
            total[key] = work_ps.tile([P, 2, n], F32, name="total", tag="work")
            nc.tensor.matmul(
                out=total[key][:].rearrange("p s n -> p (s n)"),
                lhsT=same_half[:],
                rhs=sums[key][:].rearrange("p s n -> p (s n)"),
                start=True,
                stop=True,
            )

        def means_to_sbuf(key, n):
            avg[key] = small.tile([P, 2, n], F32, name="avg")
            nc.vector.tensor_copy(out=avg[key][:], in_=total[key][:])

        def square_of_mean(key, n):
            mean_sq[key] = small.tile([P, n], F32, name="mean_sq")
            nc.vector.tensor_mul(out=mean_sq[key][:], in0=avg[key][:, 0, :], in1=avg[key][:, 0, :])

        def inverse_std(key, n, on_scalar=False):
            var_eps = small.tile([P, n], F32, name="var_eps")
            nc.vector.scalar_tensor_tensor(
                out=var_eps[:], in0=avg[key][:, 1, :], scalar=BN_EPS, in1=mean_sq[key][:],
                op0=ALU.add, op1=ALU.subtract,
            )
            rstd[key] = small.tile([P, n], F32, name="rstd")
            if on_scalar:
                nc.scalar.activation(out=rstd[key][:], in_=var_eps[:], func=ACT.Abs_reciprocal_sqrt)
            else:
                nc.gpsimd.tensor_tensor(
                    out=rstd[key][:], in0=var_eps[:], in1=minus_half[:, :n], op=ALU.pow
                )

        turned, grouped_of, codes_of, eo, gate = {}, {}, {}, {}, {}
        den_t, num_t = {}, {}

        def turn_half(k, half):
            bank, first, m = turn(rows[k][:, tile_cols(half, 2 * C)].bitcast(F32), 2)[0]
            turned.setdefault(k, []).append((bank, 2 * half, 2))

        def open_grouped(k):
            grouped_of[k] = grouped_pool.tile([P, CHUNK * C], BF16, align_bytes=64, name="grouped")

        def regroup_chunk(k, copy):
            for turned_bank in turned[k]:
                regroup(copy, turned_bank, grouped_of[k][:].bitcast(F32))

        def quantise_chunk(k):
            n = CHUNKS[k][2]
            codes_of[k] = mx_operand(codes_pool, "edge", CHUNK)
            quantise(grouped_of[k][:, : n * C], codes_of[k], slice(0, n * P))

        width = {}

        def open_sums(k, n):
            width[k] = n
            sums[k] = small.tile([P, 2, n], F32, name="sums")

        def multiply(k, pieces=((), (), (), ())):
            g, j0, n = CHUNKS[k]
            eo[k] = eo_pool.tile([P, CHUNK * C], F32, name="eo")
            for t in range(n):
                acc = agg_ps.tile([P, C], F32, name="acc", tag="agg")
                mx_pass(acc[:], codes_of[k], tile_cols(t), we, slice(0, C), True, False)
                mx_pass(acc[:], xi, tile_cols(g), wa, slice(0, C), False, False)
                mx_pass(acc[:], xj, tile_cols(j0 + t), wb, slice(0, C), False, True)
                first_moment(acc[:], eo[k][:, tile_cols(t, C)], k, t)
                for piece in pieces[t]:
                    piece()
                if not LATE(k):
                    second_moment(acc[:], k, t)
                elif t >= 1:
                    second_moment(eo[k][:, tile_cols(t - 1, C)], k, t - 1)
            if LATE(k):
                second_moment(eo[k][:, tile_cols(n - 1, C)], k, n - 1)

        def relu_centred(k, t):
            nc.vector.tensor_scalar(
                out=eo[k][:, tile_cols(t, C)], in0=eo[k][:, tile_cols(t, C)],
                scalar1=avg[k][:, 0, t : t + 1], scalar2=0.0, op0=ALU.subtract, op1=ALU.max,
            )

        def normalise(k):
            n = CHUNKS[k][2]
            square_of_mean(k, width[k])
            relu_centred(k, 0)
            inverse_std(k, width[k])

        def normalise_rest(k):
            for t in range(1, CHUNKS[k][2]):
                relu_centred(k, t)

        def add_residual(k):
            g, j0, n = CHUNKS[k]
            for t in range(n):
                nc.vector.scalar_tensor_tensor(
                    out=eo[k][:, tile_cols(t, C)], in0=eo[k][:, tile_cols(t, C)],
                    scalar=rstd[k][:, t : t + 1], in1=rows[k][:, tile_cols(t, C)],
                    op0=ALU.mult, op1=ALU.add,
                )
            nc.sync.dma_start(
                out=edge_out_rows[:, tile_cols(g * N + j0, C, n)], in_=eo[k][:, : n * C]
            )

        def gates(k):
            half = CHUNKS[k][2] * C // 2
            gate[k] = gate_pool.tile([P, 2, CHUNK * C], F32, name="gate")
            for cols in (tile_cols(0, half), tile_cols(1, half)):
                nc.scalar.activation(out=gate[k][:, 0, cols], in_=eo[k][:, cols], func=ACT.Tanh, scale=0.5)
            for cols in (tile_cols(0, half), tile_cols(1, half)):
                nc.scalar.activation(out=gate[k][:, 0, cols], in_=gate[k][:, 0, cols], func=ACT.Exp, scale=0.5)

        def weigh(engine, k, t0, n):
            cols = tile_cols(t0, C, n)
            engine.tensor_tensor(
                out=gate[k][:, 1, cols], in0=gate[k][:, 0, cols],
                in1=u_all[:, tile_cols(CHUNKS[k][1] + t0, C, n)], op=ALU.mult,
            )

        def sum_over_j(k, which=(0, 1)):
            g, j0, n = CHUNKS[k]
            if j0 == 0 and which[0] == 0:
                den_t[g] = sums_ps.tile([P, Q, P], F32, name="den_t")
                num_t[g] = sums_ps.tile([P, Q, P], F32, name="num_t")
            for s in which:
                total_t = (den_t[g], num_t[g])[s]
                for t in range(n):
                    for q in range(Q):
                        nc.tensor.matmul(
                            out=total_t[:, q, :],
                            lhsT=gate[k][:, s, t * C + q * P : t * C + (q + 1) * P],
                            rhs=ident[:],
                            is_transpose=True,
                            start=(j0 + t == 0 and q == 0),
                            stop=(j0 + t == N - 1 and q == Q - 1),
                        )

        xn_t, xn = {}, {}

        def message(g, then):
            uix_t = work_ps.tile([P, Q, P], F32, name="uix_t", tag="work")
            for q in range(Q):
                mx_pass(uix_t[:, q, :], late["wu"], tile_cols(q), xi, tile_cols(g), True, True)
            rden_t = node_pool.tile([P, Q, P], F32, name="rden_t")
            msg_t = node_pool.tile([P, Q, P], F32, name="msg_t")
            xn_t[g] = node_pool.tile([P, Q, P], F32, name="xn_t")
            nc.vector.reciprocal(out=rden_t[:], in_=den_t[g][:])
            then[0]()
            nc.vector.tensor_mul(out=msg_t[:], in0=num_t[g][:], in1=rden_t[:])
            then[1]()
            nc.vector.scalar_tensor_tensor(
                out=xn_t[g][:], in0=msg_t[:], scalar=1.0 / N, in1=uix_t[:], op0=ALU.mult, op1=ALU.add,
            )

        where = {}

        def node_moments(g, key, col):
            xn_ps = work_ps.tile([P, C], F32, name="xn_ps", tag="work")
            for q in range(Q):
                nc.tensor.transpose(xn_ps[:, tile_cols(q)], xn_t[g][:, q, :], ident[:])
            xn[g] = node_pool.tile([P, C], F32, name="xn")
            where[g] = key, col
            moments(xn_ps[:], xn[g][:], key, col)

        def node_residual(g):
            key, col = where[g]
            shift = small.tile([P, 1], F32, name="shift")
            nc.vector.scalar_tensor_tensor(
                out=shift[:], in0=avg[key][:, 0, col : col + 1], scalar=-1.0, in1=rstd[key][:, col : col + 1],
                op0=ALU.mult, op1=ALU.mult,
            )
            nc.vector.scalar_tensor_tensor(
                out=xn[g][:], in0=xn[g][:], scalar=rstd[key][:, col : col + 1],
                in1=x_own[:, tile_cols(g, C)], op0=ALU.mult, op1=ALU.add,
            )
            return shift

        def node_out(g, shift):
            xo = node_pool.tile([P, C], F32, name="xo")
            if g >= HALF - 2:
                nc.scalar.activation(out=xo[:], in_=xn[g][:], func=ACT.Relu, bias=shift[:, 0:1], scale=1.0)
            else:
                nc.gpsimd.tensor_scalar(
                    out=xo[:], in0=xn[g][:], scalar1=shift[:, 0:1], scalar2=0.0, op0=ALU.add, op1=ALU.max
                )
            nc.sync.dma_start(out=x_out_rows[:, tile_cols(g, C)], in_=xo[:])

        kept, uix_ps, rden = {}, {}, {}

        def node_sums_out(g):
            for s, total_t in enumerate((den_t[g], num_t[g])):
                kept[g, s] = node_pool.tile([P, Q, P], F32, name=("rden_t", "msg_t")[s])
                nc.vector.tensor_copy(out=kept[g, s][:], in_=total_t[:])

        def node_uix(g):
            uix_ps[g] = agg_ps.tile([P, Q, P], F32, name="uix_t", tag="agg")
            for q in range(Q):
                mx_pass(uix_ps[g][:, q, :], late["wu"], tile_cols(q), xi, tile_cols(g), True, True)
            xn_t[g] = node_pool.tile([P, Q, P], F32, name="xn_t")

        def inverse_root(g, den, qs):
            nc.scalar.activation(out=rden[g][:, qs, :], in_=den[:, qs, :], func=ACT.Abs_reciprocal_sqrt)

        def inverse(g, qs):
            nc.scalar.activation(out=rden[g][:, qs, :], in_=rden[g][:, qs, :], func=ACT.Square)

        def node_msg(g, num, qs):
            nc.vector.tensor_mul(out=rden[g][:, qs, :], in0=num[:, qs, :], in1=rden[g][:, qs, :])

        def node_add(g, qs):
            nc.vector.scalar_tensor_tensor(
                out=xn_t[g][:, qs, :], in0=rden[g][:, qs, :], scalar=1.0 / N, in1=uix_ps[g][:, qs, :],
                op0=ALU.mult, op1=ALU.add,
            )

        last = len(CHUNKS) - 1
        for i in range(-TURN, last):
            g_message = node_closed_by(i + MESSAGE)
            g_stats = node_closed_by(i + NODE_STATS)
            g_out = node_closed_by(i + NODE_OUT)
            shift = None

            if live(i + LOAD):
                load(i + LOAD)
            if i == -TURN + 1:
                wb = weight_operand("wb", wb_rows, nc.scalar.copy)
            early = g_message is not None and not live(i + TURN)
            if early and live(i):
                normalise(i)
            def quantise_next():
                if live(i + QUANTISE):
                    quantise_chunk(i + QUANTISE)

            def normalise_now():
                if live(i) and not early:
                    normalise(i)
                if live(i):
                    normalise_rest(i)

            if g_message is not None:
                message(g_message, ((quantise_next, normalise_now), (quantise_next, lambda: None))[MODE])
                if MODE == 1:
                    normalise_now()
            else:
                quantise_next()
                normalise_now()
            if live(i + MULTIPLY):
                open_sums(i + MULTIPLY, CHUNK + (g_stats is not None))
            if g_stats is not None and FIRST:
                node_moments(g_stats, i + MULTIPLY, CHUNK)
            if i == -1:
                late["wv"] = weight_operand("wv", wv_rows, nc.scalar.copy)
            if i == U_ROUNDS[-1] + 1:
                late["wu"] = weight_operand("wu", wu_rows, nc.scalar.copy)
            ks, kt = i + SUM, i + TURN
            pieces = {}
            if live(kt):
                pieces["t0"] = lambda: turn_half(kt, 0)
                pieces["t1"] = lambda: turn_half(kt, 1)
            if live(ks):
                pieces["d"] = lambda: sum_over_j(ks, (0,))
                pieces["n"] = lambda: sum_over_j(ks, (1,))
            plan = (PLANN if g_message is not None else PLAN).split("|")
            plan = [[pieces[x] for x in o.split() if x in pieces] for o in plan]
            if live(i + MULTIPLY):
                multiply(i + MULTIPLY, plan)
            else:
                for o in plan:
                    for x in o:
                        x()
            if g_stats is not None and not FIRST:
                node_moments(g_stats, i + MULTIPLY, CHUNK)
            if i == -TURN + 1:
                double_columns(CHUNK, 2)
                double_columns(CHUNK + 2, 2)
                quantise(xi_grouped[:, 4 * C :], xi, slice(4 * P, HALF * P))
                quantise_xj(1)
                double_columns(2 * CHUNK, CHUNK)
                quantise_xj(2)
            if live(i + TURN):
                open_grouped(i + TURN)
            if live(i + WEIGH):
                weigh(nc.vector, i + WEIGH, 0, CHUNK)
            if live(i + MULTIPLY):
                mean_over_graphs(i + MULTIPLY, width[i + MULTIPLY])
            if live(i + TURN):
                regroup_chunk(i + TURN, nc.scalar.copy if i + MULTIPLY < 0 else nc.vector.tensor_copy)
            if live(i + NORMALISE):
                add_residual(i + NORMALISE)
            if g_out is not None:
                shift = node_residual(g_out)
            if live(i + MULTIPLY):
                means_to_sbuf(i + MULTIPLY, width[i + MULTIPLY])
            if i in U_ROUNDS:
                make_u(i - U_ROUNDS[0])
            if live(i + GATE):
                gates(i + GATE)
            if g_out is not None:
                node_out(g_out, shift)

        closing, before = HALF - 1, HALF - 2
        every, halves = slice(0, Q), (slice(0, Q // 2), slice(Q // 2, Q))
        sum_over_j(last - 3)
        gates(last - 1)
        square_of_mean(last, width[last])
        for t in range(CHUNK):
            relu_centred(last, t)
        inverse_std(last, width[last])
        node_sums_out(before)
        add_residual(last)
        gates(last)
        weigh(nc.vector, last - 2, 0, CHUNK)
        sum_over_j(last - 2)
        shift = node_residual(before - 1)
        node_out(before - 1, shift)
        weigh(nc.vector, last - 1, 0, CHUNK)
        node_uix(before)
        node_uix(closing)
        sum_over_j(last - 1)
        sum_over_j(last, (0,))
        weigh(nc.vector, last, 0, 2)
        weigh(nc.vector, last, 2, 2)
        sum_over_j(last, (1,))
        rden[before] = kept[before, 0]
        rden[closing] = node_pool.tile([P, Q, P], F32, name="rden_t")
        inverse_root(before, kept[before, 0], every)
        inverse(before, every)
        node_msg(before, kept[before, 1], every)
        for qs in halves:
            inverse_root(closing, den_t[closing], qs)
        node_add(before, every)
        for qs in halves:
            inverse(closing, qs)
        open_sums("before", 1)
        open_sums("closing", 1)
        for qs in halves:
            node_msg(closing, num_t[closing], qs)
        for qs in halves:
            node_add(closing, qs)
        node_moments(before, "before", 0)
        node_moments(closing, "closing", 0)
        for key in ("before", "closing"):
            mean_over_graphs(key, 1)
        for key, g in (("before", before), ("closing", closing)):
            means_to_sbuf(key, 1)
            square_of_mean(key, 1)
            inverse_std(key, 1, on_scalar=True)
            shift = node_residual(g)
            node_out(g, shift)
